import numpy as np
import ml_dtypes


def mxq(x, axis, fmt="e4m3"):
    dtype, down = {"e4m3": (ml_dtypes.float8_e4m3fn, 7), "e5m2": (ml_dtypes.float8_e5m2, 14)}[fmt]
    v = np.moveaxis(np.asarray(x, np.float32).astype(ml_dtypes.bfloat16).astype(np.float64), axis, -1)
    blocks = v.reshape(v.shape[:-1] + (-1, 32))
    amax = np.abs(blocks).max(-1, keepdims=True)
    byte = np.maximum(np.where(amax > 0, np.frexp(amax)[1] - 1 + 127, 0) - down, 1)
    scale = np.exp2(byte - 127.0)
    codes = (blocks / scale).astype(np.float32).astype(dtype).astype(np.float64)
    return np.moveaxis((codes * scale).reshape(v.shape), -1, axis)


BF16 = ml_dtypes.bfloat16


def bf(x):
    return np.asarray(x, np.float32).astype(BF16)


def f64(x):
    return np.asarray(x).astype(np.float64)


B, D, HH, WW = 4, 1024, 32, 32
M = HH * WW


def setup_inputs():
    n = np.random.standard_normal((B, D, HH, WW))
    g = np.random.standard_normal((B, HH, WW))[:, None]
    a = np.random.standard_normal((B, D))[:, :, None, None]
    mu = np.random.standard_normal((B, D))[:, :, None, None]
    return {"x": bf(n + a * g + mu)}


def reference(x):
    xf = f64(x).reshape(B, D, M)
    inv_m = 1.0 / M
    xi = inv_m * xf - (inv_m * inv_m) * xf.sum(-1, keepdims=True)
    return mxq(xi, 2, "e4m3") @ mxq(xf, 2, "e4m3").transpose(0, 2, 1)

@@ -1,0 +1,215 @@
+from contextlib import ExitStack
+
+import concourse.mybir as mybir
+from concourse.masks import make_identity
+
+F32 = mybir.dt.float32
+BF16 = mybir.dt.bfloat16
+U32 = mybir.dt.uint32
+U8 = mybir.dt.uint8
+FP8X4 = mybir.dt.float8_e4m3fn_x4
+ALU = mybir.AluOpType
+
+P = 128
+B = 4
+D = 1024
+K = 1024
+INV_M = 1.0 / K
+FLOPS = 2 * B * D * D * K
+N_UNITS = 4 * B
+PINNED = True
+
+
+def v_takes_round_bank(k, j):
+    return j % 2 == 1 if k >= 13 else (k >= 2 and j == 3)
+
+
+def v_takes_unit_bank(n, tl):
+    return n >= 5 and n % 2 == 0 and tl == 3
+
+
+def round_groups(k):
+    b, i = k // 4, k % 4
+    if i < 2:
+        return [(b, 0, tl1, i) for tl1 in range(4)]
+    return [(b, 1, tl1, th2) for tl1 in (2 * (i % 2), 2 * (i % 2) + 1) for th2 in range(2)]
+
+
+def tile_covpool_pa_t_kernel(tc, x, out):
+    nc = tc.nc
+    xv = x.rearrange("b (th p tl) h w -> b th p tl (h w)", th=2, p=P, tl=4)
+    ov = out.rearrange("b (th p tl) n -> b th p tl n", th=2, p=P, tl=4)
+
+    with ExitStack() as ctx:
+        const = ctx.enter_context(tc.tile_pool(name="const", bufs=1))
+        xpool = ctx.enter_context(tc.tile_pool(name="xpool", bufs=1))
+        xipool = ctx.enter_context(tc.tile_pool(name="xipool", bufs=3))
+        gpool = ctx.enter_context(tc.tile_pool(name="gpool", bufs=4))
+        cpool = ctx.enter_context(tc.tile_pool(name="cpool", bufs=2))
+        opool = ctx.enter_context(tc.tile_pool(name="opool", bufs=6))
+        tps = ctx.enter_context(tc.psum_pool(name="tps", bufs=4))
+        aps = ctx.enter_context(tc.psum_pool(name="aps", bufs=4))
+        if PINNED:
+            ctx.enter_context(tc.manual_schedule())
+
+        ident = const.tile([P, P], F32, name="ident")
+        make_identity(nc, ident[:])
+        junk = const.tile([P, K], BF16, name="junk")
+
+        x_sb = []
+        negc = []
+        for b in range(B):
+            x_sb.append(xpool.tile([P, 8 * K], BF16, name="x%d" % b))
+            negc.append(const.tile([P, 8], F32, name="negc%d" % b))
+        for b in range(B):
+            for th in range(2):
+                dst = x_sb[b][:, th * 4 * K:(th + 1) * 4 * K].rearrange("p (tl k) -> p tl k", tl=4)
+                if b == 0 and th == 0:
+                    for tl in range(4):
+                        nc.sync.dma_start(out=dst[:, tl, :], in_=xv[b, th, :, tl, :])
+                else:
+                    nc.sync.dma_start(out=dst, in_=xv[b, th])
+
+        xi_sb = {}
+        grouped = {}
+        codes = {}
+        planes = {}
+        o_sb = {}
+
+        def sum_tile(b, th, tl):
+            t = th * 4 + tl
+            nc.vector.tensor_scalar(
+                out=junk[:], in0=x_sb[b][:, t * K:(t + 1) * K], scalar1=-(INV_M * INV_M), scalar2=None,
+                op0=ALU.mult, op1=ALU.add, accum_out=negc[b][:, t:t + 1],
+            )
+
+        def xi_tile(b, th, tl):
+            t = th * 4 + tl
+            nc.vector.tensor_scalar(
+                out=xi_sb[(b, th)][:, tl * K:(tl + 1) * K], in0=x_sb[b][:, t * K:(t + 1) * K], scalar1=INV_M,
+                scalar2=negc[b][:, t:t + 1], op0=ALU.mult, op1=ALU.add,
+            )
+
+        def form_xi(b, th, tls, alternate):
+            if (b, th) not in xi_sb:
+                xi_sb[(b, th)] = xipool.tile([P, 4 * K], BF16, name="xi")
+            if alternate:
+                for tl in tls:
+                    sum_tile(b, th, tl)
+                    xi_tile(b, th, tl)
+            else:
+                for tl in tls:
+                    sum_tile(b, th, tl)
+                for tl in tls:
+                    xi_tile(b, th, tl)
+
+        def unit(n):
+            b, i = n // 4, n % 4
+            th = i // 2
+            if i % 2 == 0:
+                words = x_sb[b][:, th * 4 * K:(th + 1) * 4 * K].bitcast(F32)
+            else:
+                words = xi_sb[(b, th)][:].bitcast(F32)
+            g_t = gpool.tile([P, 4096], BF16, name="grouped", align_bytes=64)
+            grouped[n] = g_t
+            gw = g_t[:].bitcast(F32).rearrange("p (g d u) -> p g d u", g=2, d=512, u=2)
+            for tl in range(4):
+                bank = tps.tile([P, 512], F32, name="tbank")
+                for gu in range(4):
+                    nc.tensor.transpose(
+                        bank[:, gu * P:(gu + 1) * P],
+                        words[:, tl * 512 + gu * P: tl * 512 + (gu + 1) * P],
+                        ident[:],
+                    )
+                src = bank[:].rearrange("p (g u d) -> p g d u", g=2, u=2, d=P)
+                dst = gw[:, :, tl * P:(tl + 1) * P, :]
+                if v_takes_unit_bank(n, tl):
+                    nc.vector.tensor_copy(out=dst, in_=src)
+                else:
+                    nc.scalar.copy(out=dst, in_=src)
+
+        def quantise(n):
+            i = n % 4
+            cw = cpool.tile([P, 1024], U32, name="c%d" % i, align_bytes=64)
+            sp = cpool.tile([P, 1024], U8, name="s%d" % i, align_bytes=64)
+            nc.vector.quantize_mx(out=cw[:].bitcast(FP8X4), scales=sp[:], in_=grouped[n][:])
+            codes[n] = cw
+            planes[n] = sp
+
+        def mx_group(b, th1, tl1, th2, on_vector):
+            key = (b, th1, tl1 // 2)
+            if key not in o_sb:
+                o_sb[key] = opool.tile([P, 2, D], F32, name="o")
+            o = o_sb[key]
+            n_xi, n_xf = 4 * b + 2 * th1 + 1, 4 * b + 2 * th2
+            acc = aps.tile([P, 512], F32, name="acc")
+            for g in range(2):
+                m0 = g * 512 + tl1 * P
+                nc.tensor.matmul_mx(
+                    out=acc[:],
+                    lhsT=codes[n_xi][:, m0:m0 + P].bitcast(FP8X4),
+                    lhsT_scale=planes[n_xi][:, m0:m0 + P],
+                    rhs=codes[n_xf][:, g * 512:(g + 1) * 512].bitcast(FP8X4),
+                    rhs_scale=planes[n_xf][:, g * 512:(g + 1) * 512],
+                    start=(g == 0),
+                    stop=(g == 1),
+                )
+            dst = o[:, tl1 % 2, th2 * 512:(th2 + 1) * 512].rearrange("p (q tl) -> p q tl", tl=4)
+            src = acc[:].rearrange("p (tl q) -> p q tl", tl=4)
+            if on_vector:
+                nc.vector.tensor_copy(out=dst, in_=src)
+            else:
+                nc.scalar.copy(out=dst, in_=src)
+
+        def store_pair(b, th1, pair):
+            nc.sync.dma_start(out=ov[b, th1, :, 2 * pair:2 * pair + 2, :], in_=o_sb[(b, th1, pair)][:])
+
+        def store_row(b, th1, tl1):
+            nc.sync.dma_start(out=ov[b, th1, :, tl1, :], in_=o_sb[(b, th1, tl1 // 2)][:, tl1 % 2, :])
+
+        def store_half(b, th1, pair, th2):
+            nc.sync.dma_start(
+                out=ov[b, th1, :, 2 * pair:2 * pair + 2, th2 * 512:(th2 + 1) * 512],
+                in_=o_sb[(b, th1, pair)][:, :, th2 * 512:(th2 + 1) * 512],
+            )
+
+        def mx_round(k):
+            b, i = k // 4, k % 4
+            for j, (gb, th1, tl1, th2) in enumerate(round_groups(k)):
+                mx_group(gb, th1, tl1, th2, v_takes_round_bank(k, j))
+                if k == N_UNITS - 1 and j % 2 == 1:
+                    store_row(b, th1, tl1)
+            if b == B - 1 and i < 2:
+                store_half(b, 0, 0, i)
+                store_half(b, 0, 1, i)
+            elif i == 1:
+                store_pair(b, 0, 0)
+                store_pair(b, 0, 1)
+            elif i >= 2 and k != N_UNITS - 1:
+                store_pair(b, 1, i % 2)
+
+        halves = [(m // 4, (m % 4) // 2, tls) for m in range(5, N_UNITS, 2) for tls in ((0, 1), (2, 3))]
+
+        unit(0)
+        form_xi(0, 0, (0, 1, 2, 3), True)
+        unit(1)
+        unit(2)
+        quantise(0)
+        quantise(1)
+        mx_round(0)
+        quantise(2)
+        form_xi(0, 1, (0, 1, 2, 3), True)
+        mx_round(1)
+        unit(3)
+        unit(4)
+        form_xi(halves[0][0], halves[0][1], halves[0][2], False)
+        quantise(3)
+        form_xi(halves[1][0], halves[1][1], halves[1][2], False)
+        for k in range(2, N_UNITS):
+            if k + 2 < N_UNITS:
+                quantise(k + 2)
+            if k < len(halves):
+                form_xi(halves[k][0], halves[k][1], halves[k][2], False)
+            mx_round(k)
+            if k + 3 < N_UNITS:
+                unit(k + 3)

@@ -21,11 +21,11 @@ PINNED = True
 
 
 def v_takes_round_bank(k, j):
-    return j % 2 == 1 if k >= 13 else (k >= 2 and j == 3)
+    return k >= 13 and j % 2 == 1
 
 
 def v_takes_unit_bank(n, tl):
-    return n >= 5 and n % 2 == 0 and tl == 3
+    return False
 
 
 def round_groups(k):

@@ -21,7 +21,7 @@ PINNED = True
 
 
 def v_takes_round_bank(k, j):
-    return k >= 13 and j % 2 == 1
+    return j % 2 == 1 if k >= 13 else (k >= 2 and j == 3)
 
 
 def v_takes_unit_bank(n, tl):

@@ -17,7 +17,7 @@ K = 1024
 INV_M = 1.0 / K
 FLOPS = 2 * B * D * D * K
 N_UNITS = 4 * B
-PINNED = True
+PINNED = False
 
 
 def v_takes_round_bank(k, j):

@@ -16,23 +16,21 @@ D = 1024
 K = 1024
 INV_M = 1.0 / K
 FLOPS = 2 * B * D * D * K
-N_UNITS = 4 * B
-PINNED = False
+ROUNDS = 4 * B
+XF_LEAD = 5
+ROW_STORES_FROM = 14
 
 
 def v_takes_round_bank(k, j):
-    return j % 2 == 1 if k >= 13 else (k >= 2 and j == 3)
+    return j % 2 == 1 if k >= 14 else (j == 3 and k % 4 != 1)
 
 
-def v_takes_unit_bank(n, tl):
+def v_takes_t_bank(kind, h, j):
     return False
 
 
-def round_groups(k):
-    b, i = k // 4, k % 4
-    if i < 2:
-        return [(b, 0, tl1, i) for tl1 in range(4)]
-    return [(b, 1, tl1, th2) for tl1 in (2 * (i % 2), 2 * (i % 2) + 1) for th2 in range(2)]
+def split(h):
+    return h // 4, (h % 4) // 2, h % 2
 
 
 def tile_covpool_pa_t_kernel(tc, x, out):
@@ -43,14 +41,15 @@ def tile_covpool_pa_t_kernel(tc, x, out):
     with ExitStack() as ctx:
         const = ctx.enter_context(tc.tile_pool(name="const", bufs=1))
         xpool = ctx.enter_context(tc.tile_pool(name="xpool", bufs=1))
-        xipool = ctx.enter_context(tc.tile_pool(name="xipool", bufs=3))
-        gpool = ctx.enter_context(tc.tile_pool(name="gpool", bufs=4))
-        cpool = ctx.enter_context(tc.tile_pool(name="cpool", bufs=2))
+        xipool = ctx.enter_context(tc.tile_pool(name="xipool", bufs=4))
+        gxfpool = ctx.enter_context(tc.tile_pool(name="gxfpool", bufs=2))
+        gxipool = ctx.enter_context(tc.tile_pool(name="gxipool", bufs=3))
+        cxfpool = ctx.enter_context(tc.tile_pool(name="cxfpool", bufs=2))
+        cxipool = ctx.enter_context(tc.tile_pool(name="cxipool", bufs=4))
         opool = ctx.enter_context(tc.tile_pool(name="opool", bufs=6))
         tps = ctx.enter_context(tc.psum_pool(name="tps", bufs=4))
         aps = ctx.enter_context(tc.psum_pool(name="aps", bufs=4))
-        if PINNED:
-            ctx.enter_context(tc.manual_schedule())
+        ctx.enter_context(tc.manual_schedule())
 
         ident = const.tile([P, P], F32, name="ident")
         make_identity(nc, ident[:])
@@ -64,152 +63,139 @@ def tile_covpool_pa_t_kernel(tc, x, out):
         for b in range(B):
             for th in range(2):
                 dst = x_sb[b][:, th * 4 * K:(th + 1) * 4 * K].rearrange("p (tl k) -> p tl k", tl=4)
-                if b == 0 and th == 0:
+                if b == 0:
                     for tl in range(4):
                         nc.sync.dma_start(out=dst[:, tl, :], in_=xv[b, th, :, tl, :])
                 else:
                     nc.sync.dma_start(out=dst, in_=xv[b, th])
 
         xi_sb = {}
-        grouped = {}
-        codes = {}
-        planes = {}
-        o_sb = {}
+        g_xf = {}
+        g_xi = {}
+        c_xf = {}
+        c_xi = {}
 
-        def sum_tile(b, th, tl):
-            t = th * 4 + tl
+        def sum_tile(b, t):
             nc.vector.tensor_scalar(
                 out=junk[:], in0=x_sb[b][:, t * K:(t + 1) * K], scalar1=-(INV_M * INV_M), scalar2=None,
                 op0=ALU.mult, op1=ALU.add, accum_out=negc[b][:, t:t + 1],
             )
 
-        def xi_tile(b, th, tl):
-            t = th * 4 + tl
+        def xi_tile(b, t, dst):
             nc.vector.tensor_scalar(
-                out=xi_sb[(b, th)][:, tl * K:(tl + 1) * K], in0=x_sb[b][:, t * K:(t + 1) * K], scalar1=INV_M,
+                out=dst, in0=x_sb[b][:, t * K:(t + 1) * K], scalar1=INV_M,
                 scalar2=negc[b][:, t:t + 1], op0=ALU.mult, op1=ALU.add,
             )
 
-        def form_xi(b, th, tls, alternate):
-            if (b, th) not in xi_sb:
-                xi_sb[(b, th)] = xipool.tile([P, 4 * K], BF16, name="xi")
+        def form_xi(h, alternate):
+            b, th, hf = split(h)
+            xi = xipool.tile([P, 2 * K], BF16, name="xi")
+            xi_sb[h] = xi
+            t0 = th * 4 + hf * 2
             if alternate:
-                for tl in tls:
-                    sum_tile(b, th, tl)
-                    xi_tile(b, th, tl)
+                for i in range(2):
+                    sum_tile(b, t0 + i)
+                    xi_tile(b, t0 + i, xi[:, i * K:(i + 1) * K])
             else:
-                for tl in tls:
-                    sum_tile(b, th, tl)
-                for tl in tls:
-                    xi_tile(b, th, tl)
+                for i in range(2):
+                    sum_tile(b, t0 + i)
+                for i in range(2):
+                    xi_tile(b, t0 + i, xi[:, i * K:(i + 1) * K])
 
-        def unit(n):
-            b, i = n // 4, n % 4
-            th = i // 2
-            if i % 2 == 0:
-                words = x_sb[b][:, th * 4 * K:(th + 1) * 4 * K].bitcast(F32)
-            else:
-                words = xi_sb[(b, th)][:].bitcast(F32)
-            g_t = gpool.tile([P, 4096], BF16, name="grouped", align_bytes=64)
-            grouped[n] = g_t
-            gw = g_t[:].bitcast(F32).rearrange("p (g d u) -> p g d u", g=2, d=512, u=2)
-            for tl in range(4):
-                bank = tps.tile([P, 512], F32, name="tbank")
-                for gu in range(4):
-                    nc.tensor.transpose(
-                        bank[:, gu * P:(gu + 1) * P],
-                        words[:, tl * 512 + gu * P: tl * 512 + (gu + 1) * P],
-                        ident[:],
-                    )
-                src = bank[:].rearrange("p (g u d) -> p g d u", g=2, u=2, d=P)
-                dst = gw[:, :, tl * P:(tl + 1) * P, :]
-                if v_takes_unit_bank(n, tl):
-                    nc.vector.tensor_copy(out=dst, in_=src)
-                else:
-                    nc.scalar.copy(out=dst, in_=src)
-
-        def quantise(n):
-            i = n % 4
-            cw = cpool.tile([P, 1024], U32, name="c%d" % i, align_bytes=64)
-            sp = cpool.tile([P, 1024], U8, name="s%d" % i, align_bytes=64)
-            nc.vector.quantize_mx(out=cw[:].bitcast(FP8X4), scales=sp[:], in_=grouped[n][:])
-            codes[n] = cw
-            planes[n] = sp
-
-        def mx_group(b, th1, tl1, th2, on_vector):
-            key = (b, th1, tl1 // 2)
-            if key not in o_sb:
-                o_sb[key] = opool.tile([P, 2, D], F32, name="o")
-            o = o_sb[key]
-            n_xi, n_xf = 4 * b + 2 * th1 + 1, 4 * b + 2 * th2
-            acc = aps.tile([P, 512], F32, name="acc")
-            for g in range(2):
-                m0 = g * 512 + tl1 * P
-                nc.tensor.matmul_mx(
-                    out=acc[:],
-                    lhsT=codes[n_xi][:, m0:m0 + P].bitcast(FP8X4),
-                    lhsT_scale=planes[n_xi][:, m0:m0 + P],
-                    rhs=codes[n_xf][:, g * 512:(g + 1) * 512].bitcast(FP8X4),
-                    rhs_scale=planes[n_xf][:, g * 512:(g + 1) * 512],
-                    start=(g == 0),
-                    stop=(g == 1),
-                )
-            dst = o[:, tl1 % 2, th2 * 512:(th2 + 1) * 512].rearrange("p (q tl) -> p q tl", tl=4)
-            src = acc[:].rearrange("p (tl q) -> p q tl", tl=4)
+        def transpose_tile(words, dst, on_vector):
+            bank = tps.tile([P, 512], F32, name="tbank")
+            for gu in range(4):
+                nc.tensor.transpose(bank[:, gu * P:(gu + 1) * P], words[:, gu * P:(gu + 1) * P], ident[:])
+            src = bank[:].rearrange("p (g u d) -> p g d u", g=2, u=2, d=P)
             if on_vector:
                 nc.vector.tensor_copy(out=dst, in_=src)
             else:
                 nc.scalar.copy(out=dst, in_=src)
 
-        def store_pair(b, th1, pair):
-            nc.sync.dma_start(out=ov[b, th1, :, 2 * pair:2 * pair + 2, :], in_=o_sb[(b, th1, pair)][:])
+        def transpose_xi(h):
+            g_t = gxipool.tile([P, 2048], BF16, name="g_xi", align_bytes=64)
+            g_xi[h] = g_t
+            gw = g_t[:].bitcast(F32).rearrange("p (i g d u) -> p i g d u", i=2, g=2, d=P, u=2)
+            words = xi_sb[h][:].bitcast(F32)
+            for i in range(2):
+                transpose_tile(words[:, i * 512:(i + 1) * 512], gw[:, i], v_takes_t_bank("xi", h, i))
 
-        def store_row(b, th1, tl1):
-            nc.sync.dma_start(out=ov[b, th1, :, tl1, :], in_=o_sb[(b, th1, tl1 // 2)][:, tl1 % 2, :])
+        def transpose_xf(q):
+            b, th, hf = split(q)
+            if hf == 0:
+                g_xf[(b, th)] = gxfpool.tile([P, 4096], BF16, name="g_xf", align_bytes=64)
+            gw = g_xf[(b, th)][:].bitcast(F32).rearrange("p (g d u) -> p g d u", g=2, d=512, u=2)
+            words = x_sb[b][:].bitcast(F32)
+            for i in range(2):
+                tl = hf * 2 + i
+                t = th * 4 + tl
+                transpose_tile(words[:, t * 512:(t + 1) * 512], gw[:, :, tl * P:(tl + 1) * P, :], v_takes_t_bank("xf", q, i))
 
-        def store_half(b, th1, pair, th2):
-            nc.sync.dma_start(
-                out=ov[b, th1, :, 2 * pair:2 * pair + 2, th2 * 512:(th2 + 1) * 512],
-                in_=o_sb[(b, th1, pair)][:, :, th2 * 512:(th2 + 1) * 512],
-            )
+        def quantise_xi(h):
+            cw = cxipool.tile([P, 512], U32, name="c_xi", align_bytes=64)
+            sp = cxipool.tile([P, 512], U8, name="s_xi", align_bytes=64)
+            nc.vector.quantize_mx(out=cw[:].bitcast(FP8X4), scales=sp[:], in_=g_xi[h][:])
+            c_xi[h] = (cw, sp)
+
+        def quantise_xf(b, th):
+            cw = cxfpool.tile([P, 1024], U32, name="c_xf%d" % th, align_bytes=64)
+            sp = cxfpool.tile([P, 1024], U8, name="s_xf%d" % th, align_bytes=64)
+            nc.vector.quantize_mx(out=cw[:].bitcast(FP8X4), scales=sp[:], in_=g_xf[(b, th)][:])
+            c_xf[(b, th)] = (cw, sp)
 
         def mx_round(k):
-            b, i = k // 4, k % 4
-            for j, (gb, th1, tl1, th2) in enumerate(round_groups(k)):
-                mx_group(gb, th1, tl1, th2, v_takes_round_bank(k, j))
-                if k == N_UNITS - 1 and j % 2 == 1:
-                    store_row(b, th1, tl1)
-            if b == B - 1 and i < 2:
-                store_half(b, 0, 0, i)
-                store_half(b, 0, 1, i)
-            elif i == 1:
-                store_pair(b, 0, 0)
-                store_pair(b, 0, 1)
-            elif i >= 2 and k != N_UNITS - 1:
-                store_pair(b, 1, i % 2)
+            b, th1, hf = split(k)
+            o = opool.tile([P, 2, D], F32, name="o")
+            cxi, sxi = c_xi[k]
+            for j in range(4):
+                i, th2 = j // 2, j % 2
+                cxf, sxf = c_xf[(b, th2)]
+                acc = aps.tile([P, 512], F32, name="acc")
+                for g in range(2):
+                    m0 = i * 256 + g * P
+                    nc.tensor.matmul_mx(
+                        out=acc[:],
+                        lhsT=cxi[:, m0:m0 + P].bitcast(FP8X4),
+                        lhsT_scale=sxi[:, m0:m0 + P],
+                        rhs=cxf[:, g * 512:(g + 1) * 512].bitcast(FP8X4),
+                        rhs_scale=sxf[:, g * 512:(g + 1) * 512],
+                        start=(g == 0),
+                        stop=(g == 1),
+                    )
+                dst = o[:, i, th2 * 512:(th2 + 1) * 512].rearrange("p (q tl) -> p q tl", tl=4)
+                src = acc[:].rearrange("p (tl q) -> p q tl", tl=4)
+                if v_takes_round_bank(k, j):
+                    nc.vector.tensor_copy(out=dst, in_=src)
+                else:
+                    nc.scalar.copy(out=dst, in_=src)
+                if k >= ROW_STORES_FROM and th2 == 1:
+                    nc.sync.dma_start(out=ov[b, th1, :, 2 * hf + i, :], in_=o[:, i, :])
+            if k < ROW_STORES_FROM:
+                nc.sync.dma_start(out=ov[b, th1, :, 2 * hf:2 * hf + 2, :], in_=o[:])
 
-        halves = [(m // 4, (m % 4) // 2, tls) for m in range(5, N_UNITS, 2) for tls in ((0, 1), (2, 3))]
-
-        unit(0)
-        form_xi(0, 0, (0, 1, 2, 3), True)
-        unit(1)
-        unit(2)
-        quantise(0)
-        quantise(1)
-        mx_round(0)
-        quantise(2)
-        form_xi(0, 1, (0, 1, 2, 3), True)
-        mx_round(1)
-        unit(3)
-        unit(4)
-        form_xi(halves[0][0], halves[0][1], halves[0][2], False)
-        quantise(3)
-        form_xi(halves[1][0], halves[1][1], halves[1][2], False)
-        for k in range(2, N_UNITS):
-            if k + 2 < N_UNITS:
-                quantise(k + 2)
-            if k < len(halves):
-                form_xi(halves[k][0], halves[k][1], halves[k][2], False)
+        transpose_xf(0)
+        transpose_xf(1)
+        form_xi(0, True)
+        transpose_xi(0)
+        form_xi(1, True)
+        transpose_xf(2)
+        transpose_xf(3)
+        quantise_xf(0, 0)
+        quantise_xi(0)
+        transpose_xi(1)
+        quantise_xf(0, 1)
+        for q in range(4, XF_LEAD):
+            transpose_xf(q)
+        for k in range(ROUNDS):
+            if k + 2 < ROUNDS:
+                form_xi(k + 2, False)
+            if k + 1 < ROUNDS:
+                quantise_xi(k + 1)
+            q_done = k - 1 + XF_LEAD
+            if q_done % 2 == 1 and 4 < q_done < ROUNDS:
+                quantise_xf(q_done // 4, (q_done % 4) // 2)
             mx_round(k)
-            if k + 3 < N_UNITS:
-                unit(k + 3)
+            if k + 2 < ROUNDS:
+                transpose_xi(k + 2)
+            if k + XF_LEAD < ROUNDS:
+                transpose_xf(k + XF_LEAD)

@@ -53,7 +53,7 @@ def tile_covpool_pa_t_kernel(tc, x, out):
 
         ident = const.tile([P, P], F32, name="ident")
         make_identity(nc, ident[:])
-        junk = const.tile([P, K], BF16, name="junk")
+        junk = [const.tile([P, K], BF16, name="junk%d" % i) for i in range(4)]
 
         x_sb = []
         negc = []
@@ -77,7 +77,7 @@ def tile_covpool_pa_t_kernel(tc, x, out):
 
         def sum_tile(b, t):
             nc.vector.tensor_scalar(
-                out=junk[:], in0=x_sb[b][:, t * K:(t + 1) * K], scalar1=-(INV_M * INV_M), scalar2=None,
+                out=junk[t % 4][:], in0=x_sb[b][:, t * K:(t + 1) * K], scalar1=-(INV_M * INV_M), scalar2=None,
                 op0=ALU.mult, op1=ALU.add, accum_out=negc[b][:, t:t + 1],
             )
 

@@ -22,7 +22,7 @@ ROW_STORES_FROM = 14
 
 
 def v_takes_round_bank(k, j):
-    return j % 2 == 1 if k >= 14 else (j == 3 and k % 4 != 1)
+    return j % 2 == 1 if k >= 14 else (j == 3 or (j == 1 and k % 4 == 2))
 
 
 def v_takes_t_bank(kind, h, j):

@@ -19,6 +19,7 @@ FLOPS = 2 * B * D * D * K
 ROUNDS = 4 * B
 XF_LEAD = 5
 ROW_STORES_FROM = 14
+WARM_BEFORE = 7
 
 
 def v_takes_round_bank(k, j):
@@ -54,6 +55,13 @@ def tile_covpool_pa_t_kernel(tc, x, out):
         ident = const.tile([P, P], F32, name="ident")
         make_identity(nc, ident[:])
         junk = [const.tile([P, K], BF16, name="junk%d" % i) for i in range(4)]
+        warm = const.tile([P, 512], BF16, name="warm")
+        nc.vector.memset(warm[:], 0.0)
+
+        def warm_up(n):
+            bank = aps.tile([P, 512], F32, name="acc")
+            for i in range(n):
+                nc.tensor.matmul(out=bank[:], lhsT=warm[:, 0:P], rhs=warm[:], start=True, stop=True)
 
         x_sb = []
         negc = []
@@ -173,16 +181,23 @@ def tile_covpool_pa_t_kernel(tc, x, out):
             if k < ROW_STORES_FROM:
                 nc.sync.dma_start(out=ov[b, th1, :, 2 * hf:2 * hf + 2, :], in_=o[:])
 
+        warm_up(WARM_BEFORE)
         transpose_xf(0)
+        warm_up(1)
         transpose_xf(1)
+        warm_up(1)
         form_xi(0, True)
         transpose_xi(0)
+        warm_up(1)
         form_xi(1, True)
         transpose_xf(2)
+        warm_up(1)
         transpose_xf(3)
+        warm_up(1)
         quantise_xf(0, 0)
         quantise_xi(0)
         transpose_xi(1)
+        warm_up(1)
         quantise_xf(0, 1)
         for q in range(4, XF_LEAD):
             transpose_xf(q)

@@ -18,7 +18,8 @@ INV_M = 1.0 / K
 FLOPS = 2 * B * D * D * K
 ROUNDS = 4 * B
 XF_LEAD = 5
-ROW_STORES_FROM = 14
+ROW_STORES_FROM = 12
+BANK_STORES_FROM = 14
 WARM_BEFORE = 7
 
 
@@ -176,7 +177,9 @@ def tile_covpool_pa_t_kernel(tc, x, out):
                     nc.vector.tensor_copy(out=dst, in_=src)
                 else:
                     nc.scalar.copy(out=dst, in_=src)
-                if k >= ROW_STORES_FROM and th2 == 1:
+                if k >= BANK_STORES_FROM:
+                    nc.sync.dma_start(out=ov[b, th1, :, 2 * hf + i, th2 * 512:(th2 + 1) * 512], in_=o[:, i, th2 * 512:(th2 + 1) * 512])
+                elif k >= ROW_STORES_FROM and th2 == 1:
                     nc.sync.dma_start(out=ov[b, th1, :, 2 * hf + i, :], in_=o[:, i, :])
             if k < ROW_STORES_FROM:
                 nc.sync.dma_start(out=ov[b, th1, :, 2 * hf:2 * hf + 2, :], in_=o[:])

@@ -20,7 +20,7 @@ ROUNDS = 4 * B
 XF_LEAD = 5
 ROW_STORES_FROM = 12
 BANK_STORES_FROM = 14
-WARM_BEFORE = 7
+WARM_BEFORE = 4
 
 
 def v_takes_round_bank(k, j):

from contextlib import ExitStack

import concourse.mybir as mybir
from concourse.masks import make_identity

F32 = mybir.dt.float32
BF16 = mybir.dt.bfloat16
U32 = mybir.dt.uint32
U8 = mybir.dt.uint8
FP8X4 = mybir.dt.float8_e4m3fn_x4
ALU = mybir.AluOpType

P = 128
B = 4
D = 1024
K = 1024
INV_M = 1.0 / K
FLOPS = 2 * B * D * D * K
ROUNDS = 4 * B
XF_LEAD = 5
ROW_STORES_FROM = 12
BANK_STORES_FROM = 14
WARM_BEFORE = 4


def v_takes_round_bank(k, j):
    return j % 2 == 1 if k >= 14 else (j == 3 or (j == 1 and k % 4 == 2))


def v_takes_t_bank(kind, h, j):
    return False


def split(h):
    return h // 4, (h % 4) // 2, h % 2


def tile_covpool_pa_t_kernel(tc, x, out):
    nc = tc.nc
    xv = x.rearrange("b (th p tl) h w -> b th p tl (h w)", th=2, p=P, tl=4)
    ov = out.rearrange("b (th p tl) n -> b th p tl n", th=2, p=P, tl=4)

    with ExitStack() as ctx:
        const = ctx.enter_context(tc.tile_pool(name="const", bufs=1))
        xpool = ctx.enter_context(tc.tile_pool(name="xpool", bufs=1))
        xipool = ctx.enter_context(tc.tile_pool(name="xipool", bufs=4))
        gxfpool = ctx.enter_context(tc.tile_pool(name="gxfpool", bufs=2))
        gxipool = ctx.enter_context(tc.tile_pool(name="gxipool", bufs=3))
        cxfpool = ctx.enter_context(tc.tile_pool(name="cxfpool", bufs=2))
        cxipool = ctx.enter_context(tc.tile_pool(name="cxipool", bufs=4))
        opool = ctx.enter_context(tc.tile_pool(name="opool", bufs=6))
        tps = ctx.enter_context(tc.psum_pool(name="tps", bufs=4))
        aps = ctx.enter_context(tc.psum_pool(name="aps", bufs=4))
        ctx.enter_context(tc.manual_schedule())

        ident = const.tile([P, P], F32, name="ident")
        make_identity(nc, ident[:])
        junk = [const.tile([P, K], BF16, name="junk%d" % i) for i in range(4)]
        warm = const.tile([P, 512], BF16, name="warm")
        nc.vector.memset(warm[:], 0.0)

        def warm_up(n):
            bank = aps.tile([P, 512], F32, name="acc")
            for i in range(n):
                nc.tensor.matmul(out=bank[:], lhsT=warm[:, 0:P], rhs=warm[:], start=True, stop=True)

        x_sb = []
        negc = []
        for b in range(B):
            x_sb.append(xpool.tile([P, 8 * K], BF16, name="x%d" % b))
            negc.append(const.tile([P, 8], F32, name="negc%d" % b))
        for b in range(B):
            for th in range(2):
                dst = x_sb[b][:, th * 4 * K:(th + 1) * 4 * K].rearrange("p (tl k) -> p tl k", tl=4)
                if b == 0:
                    for tl in range(4):
                        nc.sync.dma_start(out=dst[:, tl, :], in_=xv[b, th, :, tl, :])
                else:
                    nc.sync.dma_start(out=dst, in_=xv[b, th])

        xi_sb = {}
        g_xf = {}
        g_xi = {}
        c_xf = {}
        c_xi = {}

        def sum_tile(b, t):
            nc.vector.tensor_scalar(
                out=junk[t % 4][:], in0=x_sb[b][:, t * K:(t + 1) * K], scalar1=-(INV_M * INV_M), scalar2=None,
                op0=ALU.mult, op1=ALU.add, accum_out=negc[b][:, t:t + 1],
            )

        def xi_tile(b, t, dst):
            nc.vector.tensor_scalar(
                out=dst, in0=x_sb[b][:, t * K:(t + 1) * K], scalar1=INV_M,
                scalar2=negc[b][:, t:t + 1], op0=ALU.mult, op1=ALU.add,
            )

        def form_xi(h, alternate):
            b, th, hf = split(h)
            xi = xipool.tile([P, 2 * K], BF16, name="xi")
            xi_sb[h] = xi
            t0 = th * 4 + hf * 2
            if alternate:
                for i in range(2):
                    sum_tile(b, t0 + i)
                    xi_tile(b, t0 + i, xi[:, i * K:(i + 1) * K])
            else:
                for i in range(2):
                    sum_tile(b, t0 + i)
                for i in range(2):
                    xi_tile(b, t0 + i, xi[:, i * K:(i + 1) * K])

        def transpose_tile(words, dst, on_vector):
            bank = tps.tile([P, 512], F32, name="tbank")
            for gu in range(4):
                nc.tensor.transpose(bank[:, gu * P:(gu + 1) * P], words[:, gu * P:(gu + 1) * P], ident[:])
            src = bank[:].rearrange("p (g u d) -> p g d u", g=2, u=2, d=P)
            if on_vector:
                nc.vector.tensor_copy(out=dst, in_=src)
            else:
                nc.scalar.copy(out=dst, in_=src)

        def transpose_xi(h):
            g_t = gxipool.tile([P, 2048], BF16, name="g_xi", align_bytes=64)
            g_xi[h] = g_t
            gw = g_t[:].bitcast(F32).rearrange("p (i g d u) -> p i g d u", i=2, g=2, d=P, u=2)
            words = xi_sb[h][:].bitcast(F32)
            for i in range(2):
                transpose_tile(words[:, i * 512:(i + 1) * 512], gw[:, i], v_takes_t_bank("xi", h, i))

        def transpose_xf(q):
            b, th, hf = split(q)
            if hf == 0:
                g_xf[(b, th)] = gxfpool.tile([P, 4096], BF16, name="g_xf", align_bytes=64)
            gw = g_xf[(b, th)][:].bitcast(F32).rearrange("p (g d u) -> p g d u", g=2, d=512, u=2)
            words = x_sb[b][:].bitcast(F32)
            for i in range(2):
                tl = hf * 2 + i
                t = th * 4 + tl
                transpose_tile(words[:, t * 512:(t + 1) * 512], gw[:, :, tl * P:(tl + 1) * P, :], v_takes_t_bank("xf", q, i))

        def quantise_xi(h):
            cw = cxipool.tile([P, 512], U32, name="c_xi", align_bytes=64)
            sp = cxipool.tile([P, 512], U8, name="s_xi", align_bytes=64)
            nc.vector.quantize_mx(out=cw[:].bitcast(FP8X4), scales=sp[:], in_=g_xi[h][:])
            c_xi[h] = (cw, sp)

        def quantise_xf(b, th):
            cw = cxfpool.tile([P, 1024], U32, name="c_xf%d" % th, align_bytes=64)
            sp = cxfpool.tile([P, 1024], U8, name="s_xf%d" % th, align_bytes=64)
            nc.vector.quantize_mx(out=cw[:].bitcast(FP8X4), scales=sp[:], in_=g_xf[(b, th)][:])
            c_xf[(b, th)] = (cw, sp)

        def mx_round(k):
            b, th1, hf = split(k)
            o = opool.tile([P, 2, D], F32, name="o")
            cxi, sxi = c_xi[k]
            for j in range(4):
                i, th2 = j // 2, j % 2
                cxf, sxf = c_xf[(b, th2)]
                acc = aps.tile([P, 512], F32, name="acc")
                for g in range(2):
                    m0 = i * 256 + g * P
                    nc.tensor.matmul_mx(
                        out=acc[:],
                        lhsT=cxi[:, m0:m0 + P].bitcast(FP8X4),
                        lhsT_scale=sxi[:, m0:m0 + P],
                        rhs=cxf[:, g * 512:(g + 1) * 512].bitcast(FP8X4),
                        rhs_scale=sxf[:, g * 512:(g + 1) * 512],
                        start=(g == 0),
                        stop=(g == 1),
                    )
                dst = o[:, i, th2 * 512:(th2 + 1) * 512].rearrange("p (q tl) -> p q tl", tl=4)
                src = acc[:].rearrange("p (tl q) -> p q tl", tl=4)
                if v_takes_round_bank(k, j):
                    nc.vector.tensor_copy(out=dst, in_=src)
                else:
                    nc.scalar.copy(out=dst, in_=src)
                if k >= BANK_STORES_FROM:
                    nc.sync.dma_start(out=ov[b, th1, :, 2 * hf + i, th2 * 512:(th2 + 1) * 512], in_=o[:, i, th2 * 512:(th2 + 1) * 512])
                elif k >= ROW_STORES_FROM and th2 == 1:
                    nc.sync.dma_start(out=ov[b, th1, :, 2 * hf + i, :], in_=o[:, i, :])
            if k < ROW_STORES_FROM:
                nc.sync.dma_start(out=ov[b, th1, :, 2 * hf:2 * hf + 2, :], in_=o[:])

        warm_up(WARM_BEFORE)
        transpose_xf(0)
        warm_up(1)
        transpose_xf(1)
        warm_up(1)
        form_xi(0, True)
        transpose_xi(0)
        warm_up(1)
        form_xi(1, True)
        transpose_xf(2)
        warm_up(1)
        transpose_xf(3)
        warm_up(1)
        quantise_xf(0, 0)
        quantise_xi(0)
        transpose_xi(1)
        warm_up(1)
        quantise_xf(0, 1)
        for q in range(4, XF_LEAD):
            transpose_xf(q)
        for k in range(ROUNDS):
            if k + 2 < ROUNDS:
                form_xi(k + 2, False)
            if k + 1 < ROUNDS:
                quantise_xi(k + 1)
            q_done = k - 1 + XF_LEAD
            if q_done % 2 == 1 and 4 < q_done < ROUNDS:
                quantise_xf(q_done // 4, (q_done % 4) // 2)
            mx_round(k)
            if k + 2 < ROUNDS:
                transpose_xi(k + 2)
            if k + XF_LEAD < ROUNDS:
                transpose_xf(k + XF_LEAD)
